import numpy as np
import ml_dtypes


BF16 = ml_dtypes.bfloat16


def bf(x):
    return np.asarray(x, np.float32).astype(BF16)


def f64(x):
    return np.asarray(x).astype(np.float64)


E2M1 = np.array([0.0, 0.5, 1.0, 1.5, 2.0, 3.0, 4.0, 6.0, -0.0, -0.5, -1.0, -1.5, -2.0, -3.0, -4.0, -6.0])


def pack_weight(w, fmt):
    k, n = w.shape
    w = f64(bf(w)).reshape(k // 32, 32, n)
    amax = np.abs(w).max(1)
    if fmt == "e4m3":
        byte = np.frexp(amax)[1] - 1 + 127 - 7
    else:
        mant, ex = np.frexp(amax / 6.0)
        byte = np.where(mant > 0.5, ex, ex - 1) + 127
    byte = np.clip(np.where(amax > 0, byte, 1), 1, 254)
    scaled = (w * np.exp2(127.0 - byte)[:, None, :]).reshape(k, n).astype(np.float32)
    by_word = np.ascontiguousarray(scaled.reshape(k // 512, 128, 4, n).transpose(0, 1, 3, 2))
    if fmt == "e4m3":
        words = by_word.astype(ml_dtypes.float8_e4m3fn).view(np.uint8)
    else:
        c = by_word.astype(ml_dtypes.float4_e2m1fn).view(np.uint8) & 0xF
        words = c[..., 0::2] | (c[..., 1::2] << 4)
    return np.ascontiguousarray(words), np.ascontiguousarray(byte.astype(np.uint8).reshape(k // 512, 16, n))


def unpack_weight(words, scales, fmt):
    g, p, n, _ = words.shape
    if fmt == "e4m3":
        vals = np.ascontiguousarray(words).view(ml_dtypes.float8_e4m3fn).astype(np.float64)
    else:
        nib = np.empty((g, p, n, 4), np.uint8)
        nib[..., 0::2] = words & 0xF
        nib[..., 1::2] = words >> 4
        vals = E2M1[nib]
    vals = vals * np.repeat(np.exp2(scales.astype(np.float64) - 127.0), 8, axis=1)[..., None]
    return vals.transpose(0, 1, 3, 2).reshape(g * 512, n)

def pack4(w):
    words, scales = pack_weight(w, "e2m1")
    return words.reshape(words.shape[0], 128, -1), scales


def unpack4(words, scales):
    return unpack_weight(words.reshape(words.shape[0], 128, -1, 2), scales, "e2m1")


def kspread(k):
    return np.exp2(np.repeat(np.random.randint(-6, 7, k // 32), 32).astype(np.float64))


B, H, P, D, NF, DO, G = 4, 12, 8, 1536, 8, 1536, 5
N = D * H * P


def setup_inputs():
    s = kspread(D)
    x = np.random.standard_normal((B, H, P, D)) * s
    x_words, x_scales = pack4(x.reshape(B * H * P, D).T)
    lin_w = np.random.standard_normal((G * D, D)) * 0.3 / np.sqrt(D) / s
    words, scales = pack4(lin_w.T)
    return {
        "x_words": x_words,
        "x_scales": x_scales,
        "lin_w_words": words,
        "lin_w_scales": scales,
        "lin_b": bf(np.random.standard_normal(G * D) * 0.1),
        "grid": bf(np.arange(NF)[None, :] + 1.0 + 0.1 * np.random.standard_normal((G, NF))),
        "coef": bf(np.random.standard_normal((N, NF, G)) * 0.5),
        "shift": bf(np.random.standard_normal((1, H, G, P, D)) * 0.5),
    }


def reference(x_words, x_scales, lin_w_words, lin_w_scales, lin_b, grid, coef, shift):
    xq = unpack4(x_words, x_scales).T.reshape(B, H, P, D)
    xl = (xq @ unpack4(lin_w_words, lin_w_scales)) + f64(lin_b)
    xl = xl.reshape(B, G, N)
    sn = np.sin(f64(grid)[None, :, :, None] * xl[:, :, None, :])
    f = sn * f64(coef).transpose(2, 1, 0)[None]
    return f.reshape(B, H, G, NF, P, D).sum(axis=3) + f64(shift)

@@ -1,0 +1,244 @@
+import math
+from contextlib import ExitStack
+
+import concourse.mybir as mybir
+from concourse.masks import make_identity
+
+B, H, POS, D, NF, G = 4, 12, 8, 1536, 8, 5
+TOK = B * H * POS
+FLOPS = 2 * TOK * D * G * D + 4 * B * G * NF * D * H * POS
+
+F32 = mybir.dt.float32
+BF16 = mybir.dt.bfloat16
+I32 = mybir.dt.int32
+U8 = mybir.dt.uint8
+FP4X4 = mybir.dt.float4_e2m1fn_x4
+ALU = mybir.AluOpType
+ACT = mybir.ActivationFunctionType
+
+P = 128
+PASSES = D // 512
+KC = 3
+BLK = 32
+W_CHUNKS = ((0, 2), (2, 4), (4, 5))
+
+
+def tile_ka_attention_heads_mod_pa_kernel(
+    tc, x_words, x_scales, lin_w_words, lin_w_scales, lin_b, grid, coef, shift, out
+):
+    nc = tc.nc
+    steps = [(kc, j, m) for kc in range(KC) for j in range(G) for m in range(NF)]
+    n_steps = len(steps)
+    out_v = out.rearrange("b h g p d -> b (h g) (p d)").rearrange("b o (pe k l) -> b k pe o l", k=KC, l=P)
+    shift_v = shift.rearrange("u h g p d -> (u h g) (p d)").rearrange("o (pe k l) -> k pe o l", k=KC, l=P)
+    coef_v = coef.rearrange("(q a pe k l) m j -> k q (a pe) (l m j)", q=3, a=4, pe=BLK, k=KC, l=P)
+
+    with ExitStack() as ctx:
+        keep = ctx.enter_context(tc.tile_pool(name="keep", bufs=1))
+        work = ctx.enter_context(tc.tile_pool(name="work", bufs=2))
+        psum = ctx.enter_context(tc.psum_pool(name="psum", bufs=2))
+        ctx.enter_context(tc.manual_schedule())
+
+        x_codes = keep.tile([P, PASSES, 2 * TOK], U8, align_bytes=64, name="x_codes")
+        x_planes = keep.tile([P, PASSES, TOK], U8, align_bytes=64, name="x_planes")
+        w_codes, w_planes = [], []
+        for ch, (k0, k1) in enumerate(W_CHUNKS):
+            w_codes.append(keep.tile([P, PASSES, (k1 - k0) * 2 * D], U8, align_bytes=64, name="w_codes%d" % ch))
+            w_planes.append(keep.tile([P, PASSES, (k1 - k0) * D], U8, align_bytes=64, name="w_planes%d" % ch))
+        nc.vector.memset(x_planes[:].bitcast(I32), 0)
+        nc.vector.memset(w_planes[0][:].bitcast(I32), 0)
+        nc.gpsimd.memset(w_planes[1][:].bitcast(I32), 0)
+        nc.vector.memset(w_planes[2][:].bitcast(I32), 0)
+
+        def load_scales(planes, src, c0, c1):
+            for q in range(4):
+                nc.sync.dma_start(
+                    out=planes[32 * q : 32 * q + 4, :, :].bitcast(I32),
+                    in_=src[:, 4 * q : 4 * q + 4, c0:c1].rearrange("g r n -> r g n").bitcast(I32),
+                )
+
+        nc.sync.dma_start(out=x_codes[:].bitcast(I32), in_=x_words.rearrange("g p n -> p g n").bitcast(I32))
+        for ch, (k0, k1) in enumerate(W_CHUNKS):
+            nc.sync.dma_start(
+                out=w_codes[ch][:].bitcast(I32),
+                in_=lin_w_words[:, :, k0 * 2 * D : k1 * 2 * D].rearrange("g p n -> p g n").bitcast(I32),
+            )
+            if ch == 0:
+                load_scales(x_planes, x_scales, 0, TOK)
+            load_scales(w_planes[ch], lin_w_scales, k0 * D, k1 * D)
+
+        coef_t = {}
+
+        def load_coef(kc):
+            for q in range(3):
+                t = work.tile([P, P, NF, G], BF16, name="coef%d" % q)
+                nc.sync.dma_start(out=t[:].rearrange("p l m j -> p (l m j)"), in_=coef_v[kc, q])
+                coef_t[kc, q] = t
+
+        load_coef(0)
+
+        ident_b = keep.tile([P, P], BF16, name="ident_b")
+        make_identity(nc, ident_b[:])
+        ident_f = keep.tile([P, P], F32, name="ident_f")
+        make_identity(nc, ident_f[:])
+
+        grid_b = keep.tile([P, G * NF], BF16, name="grid_b")
+        nc.scalar.dma_start(out=grid_b[:], in_=grid.rearrange("j m -> (j m)").partition_broadcast(P))
+        bias_rows = keep.tile([P, P], BF16, name="bias_rows")
+        nc.vector.memset(bias_rows[:], 0.0)
+        n_blk = G * D // P
+        nc.scalar.dma_start(out=bias_rows[0:n_blk, :], in_=lin_b.rearrange("(c p) -> c p", p=P))
+        turns = keep.tile([P, G * NF], F32, name="turns")
+        nc.vector.tensor_scalar(
+            out=turns[:], in0=grid_b[:], scalar1=1.0 / (2.0 * math.pi), scalar2=None, op0=ALU.mult
+        )
+        bias_ps = psum.tile([P, P], BF16, name="coef_ps", bufs=3)
+        nc.tensor.transpose(bias_ps[:], bias_rows[:], ident_b[:])
+        bias = keep.tile([P, n_blk], F32, name="bias")
+        nc.vector.tensor_copy(out=bias[:], in_=bias_ps[:, 0:n_blk])
+
+        x_t = {}
+
+        def project(kc, k, e):
+            ch = [c for c, (k0, k1) in enumerate(W_CHUNKS) if k0 <= k < k1][0]
+            blk = 12 * (k - W_CHUNKS[ch][0]) + 3 * e + kc
+            ps = psum.tile([P, TOK], F32, name="xl_ps", bufs=3)
+            for t0, t1 in ((0, 256), (256, 384)):
+                for g in range(PASSES):
+                    nc.tensor.matmul_mx(
+                        out=ps[:, t0:t1],
+                        lhsT=w_codes[ch][:, g, 2 * P * blk : 2 * P * (blk + 1)].bitcast(FP4X4),
+                        lhsT_scale=w_planes[ch][:, g, P * blk : P * (blk + 1)],
+                        rhs=x_codes[:, g, 2 * t0 : 2 * t1].bitcast(FP4X4),
+                        rhs_scale=x_planes[:, g, t0:t1],
+                        start=(g == 0),
+                        stop=(g == PASSES - 1),
+                    )
+            return ps
+
+        def copy_out(kc, k, e, ps):
+            if (k, e) == (0, 0):
+                x_t[kc] = work.tile([P, 5 * H * POS, 4, B], F32, name="x_t")
+            col = 12 * k + 3 * e + kc
+            nc.scalar.activation(
+                out=x_t[kc][:, k : 5 * H * POS : 5, e, :],
+                in_=ps[:].rearrange("p (b r) -> p r b", b=B),
+                func=ACT.Identity,
+                bias=bias[:, col : col + 1],
+                scale=1.0,
+            )
+
+        blocks = [(k, e) for k in range(5) for e in range(4)]
+        pend = None
+        for k, e in blocks:
+            ps = project(0, k, e)
+            if pend is not None:
+                copy_out(0, *pend)
+            pend = (k, e, ps)
+        copy_out(0, *pend)
+
+        ph, cps, acc, ft, osb, sh = {}, {}, {}, {}, {}, {}
+
+        def step_round(i):
+            kc, j, m = steps[i]
+            ph[i] = work.tile([P, 12 * P], I32, name="phase", bufs=3)
+            nc.gpsimd.tensor_scalar(
+                out=ph[i][:],
+                in0=x_t[kc][:, 96 * j : 96 * (j + 1), :, :].rearrange("p c e b -> p (c e b)"),
+                scalar1=turns[:, NF * j + m : NF * j + m + 1],
+                scalar2=1.0,
+                op0=ALU.mult,
+                op1=ALU.mult,
+            )
+
+        def step_reduce(i):
+            kc, j, m = steps[i]
+            nc.vector.scalar_tensor_tensor(
+                out=ph[i][:].bitcast(F32),
+                in0=x_t[kc][:, 96 * j : 96 * (j + 1), :, :].rearrange("p c e b -> p (c e b)"),
+                scalar=turns[:, NF * j + m : NF * j + m + 1],
+                in1=ph[i][:],
+                op0=ALU.mult,
+                op1=ALU.subtract,
+            )
+
+        def step_sine(i):
+            v = ph[i][:].bitcast(F32)
+            nc.scalar.activation(out=v, in_=v, func=ACT.Sin, scale=2.0 * math.pi)
+
+        def step_coef(i):
+            kc, j, m = steps[i]
+            cps[i] = psum.tile([P, 3 * P], BF16, name="coef_ps", bufs=3)
+            for q in range(3):
+                nc.tensor.transpose(cps[i][:, P * q : P * (q + 1)], coef_t[kc, q][:, :, m, j], ident_b[:])
+
+        def step_mult(i):
+            ft[i] = work.tile([P, 12 * P], F32, name="feat", bufs=2)
+            nc.vector.tensor_tensor(
+                out=ft[i][:].rearrange("p (c b) -> p c b", b=B),
+                in0=ph[i][:].bitcast(F32).rearrange("p (c b) -> p c b", b=B),
+                in1=cps[i][:].unsqueeze(2).to_broadcast([P, 3 * P, B]),
+                op=ALU.mult,
+            )
+
+        def step_sum(i):
+            kc, j, m = steps[i]
+            if m % 2 == 0:
+                acc[i // 2] = psum.tile([P, 3, P], F32, name="acc", bufs=2)
+            for a in range(12):
+                s = (m % 2) * 12 + a
+                nc.tensor.matmul(
+                    out=acc[i // 2][:, s // 8, :],
+                    lhsT=ft[i][:, P * a : P * (a + 1)],
+                    rhs=ident_f[:],
+                    is_transpose=True,
+                    start=(s % 8 == 0),
+                    stop=(s % 8 == 7),
+                )
+
+        def load_shift(kc, h):
+            sh[kc, h] = work.tile([P, 6, P], BF16, name="sh", bufs=2)
+            for b in range(B):
+                nc.sync.dma_start(out=sh[kc, h][b:P:B, :, :], in_=shift_v[kc, :, 6 * h : 6 * h + 6, :])
+
+        def finish(tr):
+            kc, j, m = steps[2 * tr]
+            o0 = 12 * j + 3 * (m // 2)
+            h = o0 // 6
+            osb_t = work.tile([P, 3, P], F32, name="osb", bufs=3)
+            nc.vector.tensor_tensor(
+                out=osb_t[:], in0=acc[tr][:], in1=sh[kc, h][:, o0 % 6 : o0 % 6 + 3, :], op=ALU.add
+            )
+            for b in range(B):
+                nc.sync.dma_start(out=out_v[b, kc, :, o0 : o0 + 3, :], in_=osb_t[b:P:B, :, :])
+
+        project_at = {1 + (7 * n) // 4: n for n in range(20)}
+        mx_pend = None
+        for i in range(-2, n_steps + 1):
+            if 0 <= i < n_steps:
+                kc, j, m = steps[i]
+                if j == 0 and m == 0 and kc + 1 < KC:
+                    load_coef(kc + 1)
+            n = i + 2
+            if n < n_steps and n % 4 == 0:
+                load_shift(steps[n][0], (12 * steps[n][1] + 3 * (steps[n][2] // 2)) // 6)
+            if i + 2 < n_steps:
+                step_round(i + 2)
+            if 0 <= i + 1 < n_steps:
+                step_coef(i + 1)
+                step_reduce(i + 1)
+            if mx_pend is not None:
+                copy_out(*mx_pend)
+                mx_pend = None
+            if 0 <= i + 1 < n_steps:
+                step_sine(i + 1)
+            if 1 <= i and i % 2 == 0 and i >= 2:
+                finish(i // 2 - 1)
+            if 0 <= i < n_steps:
+                kc, j, m = steps[i]
+                r = NF * j + m
+                if kc + 1 < KC and r in project_at:
+                    k, e = blocks[project_at[r]]
+                    mx_pend = (kc + 1, k, e, project(kc + 1, k, e))
+                step_mult(i)
+                step_sum(i)

@@ -20,7 +20,8 @@ P = 128
 PASSES = D // 512
 KC = 3
 BLK = 32
-W_CHUNKS = ((0, 2), (2, 4), (4, 5))
+W_CHUNKS = ((0, 1), (1, 2), (2, 3), (3, 4), (4, 5))
+A_V = 9
 
 
 def tile_ka_attention_heads_mod_pa_kernel(
@@ -46,9 +47,8 @@ def tile_ka_attention_heads_mod_pa_kernel(
             w_codes.append(keep.tile([P, PASSES, (k1 - k0) * 2 * D], U8, align_bytes=64, name="w_codes%d" % ch))
             w_planes.append(keep.tile([P, PASSES, (k1 - k0) * D], U8, align_bytes=64, name="w_planes%d" % ch))
         nc.vector.memset(x_planes[:].bitcast(I32), 0)
-        nc.vector.memset(w_planes[0][:].bitcast(I32), 0)
-        nc.gpsimd.memset(w_planes[1][:].bitcast(I32), 0)
-        nc.vector.memset(w_planes[2][:].bitcast(I32), 0)
+        for ch in range(len(W_CHUNKS)):
+            nc.vector.memset(w_planes[ch][:].bitcast(I32), 0)
 
         def load_scales(planes, src, c0, c1):
             for q in range(4):
@@ -92,17 +92,20 @@ def tile_ka_attention_heads_mod_pa_kernel(
         nc.vector.tensor_scalar(
             out=turns[:], in0=grid_b[:], scalar1=1.0 / (2.0 * math.pi), scalar2=None, op0=ALU.mult
         )
-        bias_ps = psum.tile([P, P], BF16, name="coef_ps", bufs=3)
+        bias_ps = psum.tile([P, P], BF16, name="coef_ps", bufs=2)
+        warm = keep.tile([P, 1], F32, name="warm")
+        nc.vector.memset(warm[:], 0.0)
+        nc.scalar.activation(out=warm[:], in_=warm[:], func=ACT.Sin, scale=1.0)
         nc.tensor.transpose(bias_ps[:], bias_rows[:], ident_b[:])
         bias = keep.tile([P, n_blk], F32, name="bias")
         nc.vector.tensor_copy(out=bias[:], in_=bias_ps[:, 0:n_blk])
 
         x_t = {}
 
-        def project(kc, k, e):
+        def project(kc, k, e, bank="xl"):
             ch = [c for c, (k0, k1) in enumerate(W_CHUNKS) if k0 <= k < k1][0]
             blk = 12 * (k - W_CHUNKS[ch][0]) + 3 * e + kc
-            ps = psum.tile([P, TOK], F32, name="xl_ps", bufs=3)
+            ps = psum.tile([P, TOK], F32, name=bank, bufs=1)
             for t0, t1 in ((0, 256), (256, 384)):
                 for g in range(PASSES):
                     nc.tensor.matmul_mx(
@@ -131,17 +134,17 @@ def tile_ka_attention_heads_mod_pa_kernel(
         blocks = [(k, e) for k in range(5) for e in range(4)]
         pend = None
         for k, e in blocks:
-            ps = project(0, k, e)
+            ps = project(0, k, e, ("xl", "xp0", "xp1", "xp2")[e])
             if pend is not None:
                 copy_out(0, *pend)
             pend = (k, e, ps)
         copy_out(0, *pend)
 
-        ph, cps, acc, ft, osb, sh = {}, {}, {}, {}, {}, {}
+        ph, cps, csb, acc, ft, fp, sh, x_ps = {}, {}, {}, {}, {}, {}, {}, {}
 
         def step_round(i):
             kc, j, m = steps[i]
-            ph[i] = work.tile([P, 12 * P], I32, name="phase", bufs=3)
+            ph[i] = work.tile([P, 12 * P], I32, name="phase", bufs=4)
             nc.gpsimd.tensor_scalar(
                 out=ph[i][:],
                 in0=x_t[kc][:, 96 * j : 96 * (j + 1), :, :].rearrange("p c e b -> p (c e b)"),
@@ -153,14 +156,28 @@ def tile_ka_attention_heads_mod_pa_kernel(
 
         def step_reduce(i):
             kc, j, m = steps[i]
-            nc.vector.scalar_tensor_tensor(
-                out=ph[i][:].bitcast(F32),
-                in0=x_t[kc][:, 96 * j : 96 * (j + 1), :, :].rearrange("p c e b -> p (c e b)"),
-                scalar=turns[:, NF * j + m : NF * j + m + 1],
-                in1=ph[i][:],
-                op0=ALU.mult,
-                op1=ALU.subtract,
-            )
+            for q in range(3):
+                cols = slice(512 * q, 512 * (q + 1))
+                nc.vector.scalar_tensor_tensor(
+                    out=ph[i][:, cols].bitcast(F32),
+                    in0=x_ps[q][:],
+                    scalar=turns[:, NF * j + m : NF * j + m + 1],
+                    in1=ph[i][:, cols],
+                    op0=ALU.mult,
+                    op1=ALU.subtract,
+                )
+
+        def load_x(i):
+            kc, j, m = steps[i]
+            for q in range(3):
+                x_ps[q] = psum.tile([P, 512], F32, name="xp%d" % q, bufs=1)
+                nc.tensor.matmul(
+                    out=x_ps[q][:],
+                    lhsT=ident_f[:],
+                    rhs=x_t[kc][:, 96 * j + 32 * q : 96 * j + 32 * (q + 1), :, :].rearrange("p c e b -> p (c e b)"),
+                    start=True,
+                    stop=True,
+                )
 
         def step_sine(i):
             v = ph[i][:].bitcast(F32)
@@ -168,16 +185,31 @@ def tile_ka_attention_heads_mod_pa_kernel(
 
         def step_coef(i):
             kc, j, m = steps[i]
-            cps[i] = psum.tile([P, 3 * P], BF16, name="coef_ps", bufs=3)
+            cps[i] = psum.tile([P, 3 * P], BF16, name="coef_ps", bufs=2)
             for q in range(3):
                 nc.tensor.transpose(cps[i][:, P * q : P * (q + 1)], coef_t[kc, q][:, :, m, j], ident_b[:])
 
+        n_v, n_p = BLK * A_V, BLK * (12 - A_V)
+
+        def copy_coef(i):
+            csb[i] = work.tile([P, n_p], BF16, name="csb", bufs=2)
+            nc.scalar.copy(out=csb[i][:], in_=cps[i][:, n_v:])
+
         def step_mult(i):
-            ft[i] = work.tile([P, 12 * P], F32, name="feat", bufs=2)
+            ft[i] = work.tile([P, B * n_v], F32, name="feat_v", bufs=2)
             nc.vector.tensor_tensor(
                 out=ft[i][:].rearrange("p (c b) -> p c b", b=B),
-                in0=ph[i][:].bitcast(F32).rearrange("p (c b) -> p c b", b=B),
-                in1=cps[i][:].unsqueeze(2).to_broadcast([P, 3 * P, B]),
+                in0=ph[i][:, 0 : B * n_v].bitcast(F32).rearrange("p (c b) -> p c b", b=B),
+                in1=cps[i][:, 0:n_v].unsqueeze(2).to_broadcast([P, n_v, B]),
+                op=ALU.mult,
+            )
+
+        def step_mult_p(i):
+            fp[i] = work.tile([P, B * n_p], F32, name="feat_p", bufs=2)
+            nc.gpsimd.tensor_tensor(
+                out=fp[i][:].rearrange("p (c b) -> p c b", b=B),
+                in0=ph[i][:, B * n_v :].bitcast(F32).rearrange("p (c b) -> p c b", b=B),
+                in1=csb[i][:].unsqueeze(2).to_broadcast([P, n_p, B]),
                 op=ALU.mult,
             )
 
@@ -189,7 +221,7 @@ def tile_ka_attention_heads_mod_pa_kernel(
                 s = (m % 2) * 12 + a
                 nc.tensor.matmul(
                     out=acc[i // 2][:, s // 8, :],
-                    lhsT=ft[i][:, P * a : P * (a + 1)],
+                    lhsT=ft[i][:, P * a : P * (a + 1)] if a < A_V else fp[i][:, P * (a - A_V) : P * (a - A_V + 1)],
                     rhs=ident_f[:],
                     is_transpose=True,
                     start=(s % 8 == 0),
@@ -214,16 +246,20 @@ def tile_ka_attention_heads_mod_pa_kernel(
 
         project_at = {1 + (7 * n) // 4: n for n in range(20)}
         mx_pend = None
-        for i in range(-2, n_steps + 1):
+        for i in range(-3, n_steps + 1):
             if 0 <= i < n_steps:
                 kc, j, m = steps[i]
                 if j == 0 and m == 0 and kc + 1 < KC:
                     load_coef(kc + 1)
             n = i + 2
-            if n < n_steps and n % 4 == 0:
+            if 0 <= n < n_steps and n % 4 == 0:
                 load_shift(steps[n][0], (12 * steps[n][1] + 3 * (steps[n][2] // 2)) // 6)
-            if i + 2 < n_steps:
-                step_round(i + 2)
+            if 0 <= i < n_steps:
+                step_mult_p(i)
+            if i + 3 < n_steps:
+                step_round(i + 3)
+            if i == -2:
+                load_x(0)
             if 0 <= i + 1 < n_steps:
                 step_coef(i + 1)
                 step_reduce(i + 1)
@@ -231,12 +267,15 @@ def tile_ka_attention_heads_mod_pa_kernel(
                 copy_out(*mx_pend)
                 mx_pend = None
             if 0 <= i + 1 < n_steps:
+                copy_coef(i + 1)
                 step_sine(i + 1)
-            if 1 <= i and i % 2 == 0 and i >= 2:
+            if i >= 2 and i % 2 == 0:
                 finish(i // 2 - 1)
             if 0 <= i < n_steps:
                 kc, j, m = steps[i]
                 r = NF * j + m
+                if i + 2 < n_steps and steps[i + 2][2] == 0:
+                    load_x(i + 2)
                 if kc + 1 < KC and r in project_at:
                     k, e = blocks[project_at[r]]
                     mx_pend = (kc + 1, k, e, project(kc + 1, k, e))

@@ -21,7 +21,7 @@ PASSES = D // 512
 KC = 3
 BLK = 32
 W_CHUNKS = ((0, 1), (1, 2), (2, 3), (3, 4), (4, 5))
-A_V = 9
+A_V = 10
 
 
 def tile_ka_attention_heads_mod_pa_kernel(
@@ -140,7 +140,7 @@ def tile_ka_attention_heads_mod_pa_kernel(
             pend = (k, e, ps)
         copy_out(0, *pend)
 
-        ph, cps, csb, acc, ft, fp, sh, x_ps = {}, {}, {}, {}, {}, {}, {}, {}
+        ph, cps, csb, acc, ft, fp, sh, shx, x_ps = {}, {}, {}, {}, {}, {}, {}, {}, {}
 
         def step_round(i):
             kc, j, m = steps[i]
@@ -149,9 +149,9 @@ def tile_ka_attention_heads_mod_pa_kernel(
                 out=ph[i][:],
                 in0=x_t[kc][:, 96 * j : 96 * (j + 1), :, :].rearrange("p c e b -> p (c e b)"),
                 scalar1=turns[:, NF * j + m : NF * j + m + 1],
-                scalar2=1.0,
+                scalar2=0.0,
                 op0=ALU.mult,
-                op1=ALU.mult,
+                op1=ALU.add,
             )
 
         def step_reduce(i):
@@ -219,65 +219,99 @@ def tile_ka_attention_heads_mod_pa_kernel(
                 acc[i // 2] = psum.tile([P, 3, P], F32, name="acc", bufs=2)
             for a in range(12):
                 s = (m % 2) * 12 + a
+                if s % 8 == 0:
+                    o = (12 * i + a) // 8
+                    nc.tensor.matmul(
+                        out=acc[i // 2][:, s // 8, :],
+                        lhsT=shx[o // 4][:, o % 4, :, :].rearrange("p c b -> p (c b)"),
+                        rhs=ident_f[:],
+                        is_transpose=True,
+                        start=True,
+                        stop=False,
+                    )
                 nc.tensor.matmul(
                     out=acc[i // 2][:, s // 8, :],
                     lhsT=ft[i][:, P * a : P * (a + 1)] if a < A_V else fp[i][:, P * (a - A_V) : P * (a - A_V + 1)],
                     rhs=ident_f[:],
                     is_transpose=True,
-                    start=(s % 8 == 0),
+                    start=False,
                     stop=(s % 8 == 7),
                 )
 
-        def load_shift(kc, h):
-            sh[kc, h] = work.tile([P, 6, P], BF16, name="sh", bufs=2)
-            for b in range(B):
-                nc.sync.dma_start(out=sh[kc, h][b:P:B, :, :], in_=shift_v[kc, :, 6 * h : 6 * h + 6, :])
+        def load_shift(n):
+            sh[n] = work.tile([P, 3, P], BF16, name="sh", bufs=2)
+            kc, j = divmod(n, G)
+            for r in range(4):
+                nc.sync.dma_start(
+                    out=sh[n][BLK * r : BLK * (r + 1), :, :],
+                    in_=shift_v[kc, :, 12 * j + r : 12 * (j + 1) : 4, :],
+                )
+
+        def turn_shift(n):
+            sps = psum.tile([P, P], BF16, name="xl", bufs=1)
+            nc.tensor.transpose(sps[:], sh[n // 3][:, n % 3, :], ident_b[:])
+            return sps
+
+        def spread_shift(n, sps):
+            shx[n] = work.tile([P, 4, BLK, B], F32, name="shx", bufs=2)
+            nc.scalar.activation(
+                out=shx[n][:].rearrange("p o c b -> p (o c) b"),
+                in_=sps[:].unsqueeze(2).to_broadcast([P, P, B]),
+                func=ACT.Copy,
+                scale=1.0,
+            )
 
         def finish(tr):
             kc, j, m = steps[2 * tr]
             o0 = 12 * j + 3 * (m // 2)
-            h = o0 // 6
-            osb_t = work.tile([P, 3, P], F32, name="osb", bufs=3)
-            nc.vector.tensor_tensor(
-                out=osb_t[:], in0=acc[tr][:], in1=sh[kc, h][:, o0 % 6 : o0 % 6 + 3, :], op=ALU.add
-            )
+            osb_t = work.tile([P, 3, P], F32, name="osb", bufs=2)
+            nc.scalar.copy(out=osb_t[:], in_=acc[tr][:])
             for b in range(B):
                 nc.sync.dma_start(out=out_v[b, kc, :, o0 : o0 + 3, :], in_=osb_t[b:P:B, :, :])
 
-        project_at = {1 + (7 * n) // 4: n for n in range(20)}
-        mx_pend = None
-        for i in range(-3, n_steps + 1):
+        n_quads = n_steps * 12 // 32
+        shift_at = {(32 * n) // 12 - 3: n for n in range(n_quads)}
+        project_at = {}
+        for kc in range(1, KC):
+            free = [i for i in range(40 * (kc - 1), 40 * kc - 5) if i not in shift_at]
+            for n in range(len(blocks)):
+                project_at[free[n]] = (kc,) + blocks[n]
+        x_pend, s_pend = None, None
+        for i in range(-4, n_steps + 1):
             if 0 <= i < n_steps:
                 kc, j, m = steps[i]
                 if j == 0 and m == 0 and kc + 1 < KC:
                     load_coef(kc + 1)
-            n = i + 2
-            if 0 <= n < n_steps and n % 4 == 0:
-                load_shift(steps[n][0], (12 * steps[n][1] + 3 * (steps[n][2] // 2)) // 6)
+            if i == -4:
+                load_shift(0)
+            if i >= 0 and i % 8 == 0 and i + 8 < n_steps:
+                load_shift(i // 8 + 1)
             if 0 <= i < n_steps:
                 step_mult_p(i)
-            if i + 3 < n_steps:
+            if 0 <= i + 3 < n_steps:
                 step_round(i + 3)
             if i == -2:
                 load_x(0)
             if 0 <= i + 1 < n_steps:
                 step_coef(i + 1)
                 step_reduce(i + 1)
-            if mx_pend is not None:
-                copy_out(*mx_pend)
-                mx_pend = None
+            if x_pend is not None:
+                copy_out(*x_pend)
+                x_pend = None
+            if s_pend is not None:
+                spread_shift(*s_pend)
+                s_pend = None
+            if i >= 2 and i % 2 == 0:
+                finish(i // 2 - 1)
             if 0 <= i + 1 < n_steps:
                 copy_coef(i + 1)
                 step_sine(i + 1)
-            if i >= 2 and i % 2 == 0:
-                finish(i // 2 - 1)
+            if i in shift_at:
+                s_pend = (shift_at[i], turn_shift(shift_at[i]))
+            if i in project_at:
+                x_pend = project_at[i] + (project(*project_at[i]),)
             if 0 <= i < n_steps:
-                kc, j, m = steps[i]
-                r = NF * j + m
                 if i + 2 < n_steps and steps[i + 2][2] == 0:
                     load_x(i + 2)
-                if kc + 1 < KC and r in project_at:
-                    k, e = blocks[project_at[r]]
-                    mx_pend = (kc + 1, k, e, project(kc + 1, k, e))
                 step_mult(i)
                 step_sum(i)

@@ -46,26 +46,28 @@ def tile_ka_attention_heads_mod_pa_kernel(
         for ch, (k0, k1) in enumerate(W_CHUNKS):
             w_codes.append(keep.tile([P, PASSES, (k1 - k0) * 2 * D], U8, align_bytes=64, name="w_codes%d" % ch))
             w_planes.append(keep.tile([P, PASSES, (k1 - k0) * D], U8, align_bytes=64, name="w_planes%d" % ch))
+        nc.gpsimd.memset(w_planes[0][:].bitcast(I32), 0)
         nc.vector.memset(x_planes[:].bitcast(I32), 0)
-        for ch in range(len(W_CHUNKS)):
+        for ch in range(1, len(W_CHUNKS)):
             nc.vector.memset(w_planes[ch][:].bitcast(I32), 0)
 
-        def load_scales(planes, src, c0, c1):
-            for q in range(4):
+        def load_scales(planes, src, c0, c1, quads=range(4)):
+            for q in quads:
                 nc.sync.dma_start(
                     out=planes[32 * q : 32 * q + 4, :, :].bitcast(I32),
                     in_=src[:, 4 * q : 4 * q + 4, c0:c1].rearrange("g r n -> r g n").bitcast(I32),
                 )
 
         nc.sync.dma_start(out=x_codes[:].bitcast(I32), in_=x_words.rearrange("g p n -> p g n").bitcast(I32))
+        load_scales(x_planes, x_scales, 0, TOK)
         for ch, (k0, k1) in enumerate(W_CHUNKS):
+            if ch == 0:
+                load_scales(w_planes[ch], lin_w_scales, k0 * D, k1 * D, range(2))
             nc.sync.dma_start(
                 out=w_codes[ch][:].bitcast(I32),
                 in_=lin_w_words[:, :, k0 * 2 * D : k1 * 2 * D].rearrange("g p n -> p g n").bitcast(I32),
             )
-            if ch == 0:
-                load_scales(x_planes, x_scales, 0, TOK)
-            load_scales(w_planes[ch], lin_w_scales, k0 * D, k1 * D)
+            load_scales(w_planes[ch], lin_w_scales, k0 * D, k1 * D, range(2, 4) if ch == 0 else range(4))
 
         coef_t = {}
 
@@ -83,11 +85,11 @@ def tile_ka_attention_heads_mod_pa_kernel(
         make_identity(nc, ident_f[:])
 
         grid_b = keep.tile([P, G * NF], BF16, name="grid_b")
-        nc.scalar.dma_start(out=grid_b[:], in_=grid.rearrange("j m -> (j m)").partition_broadcast(P))
+        nc.gpsimd.dma_start(out=grid_b[:], in_=grid.rearrange("j m -> (j m)").partition_broadcast(P))
         bias_rows = keep.tile([P, P], BF16, name="bias_rows")
         nc.vector.memset(bias_rows[:], 0.0)
         n_blk = G * D // P
-        nc.scalar.dma_start(out=bias_rows[0:n_blk, :], in_=lin_b.rearrange("(c p) -> c p", p=P))
+        nc.gpsimd.dma_start(out=bias_rows[0:n_blk, :], in_=lin_b.rearrange("(c p) -> c p", p=P))
         turns = keep.tile([P, G * NF], F32, name="turns")
         nc.vector.tensor_scalar(
             out=turns[:], in0=grid_b[:], scalar1=1.0 / (2.0 * math.pi), scalar2=None, op0=ALU.mult
@@ -96,16 +98,14 @@ def tile_ka_attention_heads_mod_pa_kernel(
         warm = keep.tile([P, 1], F32, name="warm")
         nc.vector.memset(warm[:], 0.0)
         nc.scalar.activation(out=warm[:], in_=warm[:], func=ACT.Sin, scale=1.0)
-        nc.tensor.transpose(bias_ps[:], bias_rows[:], ident_b[:])
         bias = keep.tile([P, n_blk], F32, name="bias")
-        nc.vector.tensor_copy(out=bias[:], in_=bias_ps[:, 0:n_blk])
 
         x_t = {}
 
         def project(kc, k, e, bank="xl"):
             ch = [c for c, (k0, k1) in enumerate(W_CHUNKS) if k0 <= k < k1][0]
             blk = 12 * (k - W_CHUNKS[ch][0]) + 3 * e + kc
-            ps = psum.tile([P, TOK], F32, name=bank, bufs=1)
+            ps = psum.tile([P, TOK], F32, name=bank, bufs=4 if bank == "xp" else 1)
             for t0, t1 in ((0, 256), (256, 384)):
                 for g in range(PASSES):
                     nc.tensor.matmul_mx(
@@ -134,7 +134,10 @@ def tile_ka_attention_heads_mod_pa_kernel(
         blocks = [(k, e) for k in range(5) for e in range(4)]
         pend = None
         for k, e in blocks:
-            ps = project(0, k, e, ("xl", "xp0", "xp1", "xp2")[e])
+            ps = project(0, k, e, "xl" if e == 0 else "xp")
+            if (k, e) == (0, 1):
+                nc.tensor.transpose(bias_ps[:], bias_rows[:], ident_b[:])
+                nc.vector.tensor_copy(out=bias[:], in_=bias_ps[:, 0:n_blk])
             if pend is not None:
                 copy_out(0, *pend)
             pend = (k, e, ps)
@@ -142,17 +145,23 @@ def tile_ka_attention_heads_mod_pa_kernel(
 
         ph, cps, csb, acc, ft, fp, sh, shx, x_ps = {}, {}, {}, {}, {}, {}, {}, {}, {}
 
+        def pieces(i):
+            return ((0, 4), (4, 8), (8, 12)) if i == 0 else ((0, 12),)
+
         def step_round(i):
             kc, j, m = steps[i]
             ph[i] = work.tile([P, 12 * P], I32, name="phase", bufs=4)
-            nc.gpsimd.tensor_scalar(
-                out=ph[i][:],
-                in0=x_t[kc][:, 96 * j : 96 * (j + 1), :, :].rearrange("p c e b -> p (c e b)"),
-                scalar1=turns[:, NF * j + m : NF * j + m + 1],
-                scalar2=0.0,
-                op0=ALU.mult,
-                op1=ALU.add,
-            )
+            for a0, a1 in pieces(i):
+                nc.gpsimd.tensor_scalar(
+                    out=ph[i][:, P * a0 : P * a1].rearrange("p (a b c) -> p a b c", b=B, c=BLK),
+                    in0=x_t[kc][:, 96 * j + POS * a0 : 96 * j + POS * a1, :, :].rearrange(
+                        "p (a q) e b -> p a b (q e)", q=POS
+                    ),
+                    scalar1=turns[:, NF * j + m : NF * j + m + 1],
+                    scalar2=0.0,
+                    op0=ALU.mult,
+                    op1=ALU.add,
+                )
 
         def step_reduce(i):
             kc, j, m = steps[i]
@@ -160,28 +169,31 @@ def tile_ka_attention_heads_mod_pa_kernel(
                 cols = slice(512 * q, 512 * (q + 1))
                 nc.vector.scalar_tensor_tensor(
                     out=ph[i][:, cols].bitcast(F32),
-                    in0=x_ps[q][:],
+                    in0=x_ps[i // NF, q][:],
                     scalar=turns[:, NF * j + m : NF * j + m + 1],
                     in1=ph[i][:, cols],
                     op0=ALU.mult,
                     op1=ALU.subtract,
                 )
 
-        def load_x(i):
+        def load_x(i, thirds):
             kc, j, m = steps[i]
-            for q in range(3):
-                x_ps[q] = psum.tile([P, 512], F32, name="xp%d" % q, bufs=1)
+            for q in thirds:
+                x_ps[i // NF, q] = psum.tile([P, 512], F32, name="xp", bufs=4)
                 nc.tensor.matmul(
-                    out=x_ps[q][:],
+                    out=x_ps[i // NF, q][:].rearrange("p (a b c) -> p a b c", b=B, c=BLK),
                     lhsT=ident_f[:],
-                    rhs=x_t[kc][:, 96 * j + 32 * q : 96 * j + 32 * (q + 1), :, :].rearrange("p c e b -> p (c e b)"),
+                    rhs=x_t[kc][:, 96 * j + 32 * q : 96 * j + 32 * (q + 1), :, :].rearrange(
+                        "p (a q) e b -> p a b (q e)", q=POS
+                    ),
                     start=True,
                     stop=True,
                 )
 
         def step_sine(i):
-            v = ph[i][:].bitcast(F32)
-            nc.scalar.activation(out=v, in_=v, func=ACT.Sin, scale=2.0 * math.pi)
+            for a0, a1 in pieces(i):
+                v = ph[i][:, P * a0 : P * a1].bitcast(F32)
+                nc.scalar.activation(out=v, in_=v, func=ACT.Sin, scale=2.0 * math.pi)
 
         def step_coef(i):
             kc, j, m = steps[i]
@@ -198,32 +210,32 @@ def tile_ka_attention_heads_mod_pa_kernel(
         def step_mult(i):
             ft[i] = work.tile([P, B * n_v], F32, name="feat_v", bufs=2)
             nc.vector.tensor_tensor(
-                out=ft[i][:].rearrange("p (c b) -> p c b", b=B),
-                in0=ph[i][:, 0 : B * n_v].bitcast(F32).rearrange("p (c b) -> p c b", b=B),
-                in1=cps[i][:, 0:n_v].unsqueeze(2).to_broadcast([P, n_v, B]),
+                out=ft[i][:].rearrange("p (a b c) -> p a b c", b=B, c=BLK),
+                in0=ph[i][:, 0 : B * n_v].bitcast(F32).rearrange("p (a b c) -> p a b c", b=B, c=BLK),
+                in1=cps[i][:, 0:n_v].rearrange("p (a c) -> p a c", c=BLK).unsqueeze(2).to_broadcast([P, A_V, B, BLK]),
                 op=ALU.mult,
             )
 
         def step_mult_p(i):
             fp[i] = work.tile([P, B * n_p], F32, name="feat_p", bufs=2)
             nc.gpsimd.tensor_tensor(
-                out=fp[i][:].rearrange("p (c b) -> p c b", b=B),
-                in0=ph[i][:, B * n_v :].bitcast(F32).rearrange("p (c b) -> p c b", b=B),
-                in1=csb[i][:].unsqueeze(2).to_broadcast([P, n_p, B]),
+                out=fp[i][:].rearrange("p (a b c) -> p a b c", b=B, c=BLK),
+                in0=ph[i][:, B * n_v :].bitcast(F32).rearrange("p (a b c) -> p a b c", b=B, c=BLK),
+                in1=csb[i][:].rearrange("p (a c) -> p a c", c=BLK).unsqueeze(2).to_broadcast([P, 12 - A_V, B, BLK]),
                 op=ALU.mult,
             )
 
         def step_sum(i):
             kc, j, m = steps[i]
             if m % 2 == 0:
-                acc[i // 2] = psum.tile([P, 3, P], F32, name="acc", bufs=2)
+                acc[i // 2] = psum.tile([P, 3, P], F32, name="acc", bufs=1)
             for a in range(12):
                 s = (m % 2) * 12 + a
                 if s % 8 == 0:
                     o = (12 * i + a) // 8
                     nc.tensor.matmul(
                         out=acc[i // 2][:, s // 8, :],
-                        lhsT=shx[o // 4][:, o % 4, :, :].rearrange("p c b -> p (c b)"),
+                        lhsT=shx[o // 4][:, o % 4, :, :].rearrange("p b c -> p (b c)"),
                         rhs=ident_f[:],
                         is_transpose=True,
                         start=True,
@@ -253,10 +265,10 @@ def tile_ka_attention_heads_mod_pa_kernel(
             return sps
 
         def spread_shift(n, sps):
-            shx[n] = work.tile([P, 4, BLK, B], F32, name="shx", bufs=2)
+            shx[n] = work.tile([P, 4, B, BLK], F32, name="shx", bufs=2)
             nc.scalar.activation(
-                out=shx[n][:].rearrange("p o c b -> p (o c) b"),
-                in_=sps[:].unsqueeze(2).to_broadcast([P, P, B]),
+                out=shx[n][:],
+                in_=sps[:].rearrange("p (o c) -> p o c", c=BLK).unsqueeze(2).to_broadcast([P, 4, B, BLK]),
                 func=ACT.Copy,
                 scale=1.0,
             )
@@ -267,7 +279,7 @@ def tile_ka_attention_heads_mod_pa_kernel(
             osb_t = work.tile([P, 3, P], F32, name="osb", bufs=2)
             nc.scalar.copy(out=osb_t[:], in_=acc[tr][:])
             for b in range(B):
-                nc.sync.dma_start(out=out_v[b, kc, :, o0 : o0 + 3, :], in_=osb_t[b:P:B, :, :])
+                nc.sync.dma_start(out=out_v[b, kc, :, o0 : o0 + 3, :], in_=osb_t[BLK * b : BLK * (b + 1), :, :])
 
         n_quads = n_steps * 12 // 32
         shift_at = {(32 * n) // 12 - 3: n for n in range(n_quads)}
@@ -291,7 +303,7 @@ def tile_ka_attention_heads_mod_pa_kernel(
             if 0 <= i + 3 < n_steps:
                 step_round(i + 3)
             if i == -2:
-                load_x(0)
+                load_x(0, range(3))
             if 0 <= i + 1 < n_steps:
                 step_coef(i + 1)
                 step_reduce(i + 1)
@@ -312,6 +324,8 @@ def tile_ka_attention_heads_mod_pa_kernel(
                 x_pend = project_at[i] + (project(*project_at[i]),)
             if 0 <= i < n_steps:
                 if i + 2 < n_steps and steps[i + 2][2] == 0:
-                    load_x(i + 2)
+                    load_x(i + 2, range(1, 3))
+                if i + 3 < n_steps and steps[i + 3][2] == 0:
+                    load_x(i + 3, range(1))
                 step_mult(i)
                 step_sum(i)

@@ -105,7 +105,7 @@ def tile_ka_attention_heads_mod_pa_kernel(
         def project(kc, k, e, bank="xl"):
             ch = [c for c, (k0, k1) in enumerate(W_CHUNKS) if k0 <= k < k1][0]
             blk = 12 * (k - W_CHUNKS[ch][0]) + 3 * e + kc
-            ps = psum.tile([P, TOK], F32, name=bank, bufs=4 if bank == "xp" else 1)
+            ps = psum.tile([P, TOK], F32, name=bank, bufs=3 if bank == "xp" else 1)
             for t0, t1 in ((0, 256), (256, 384)):
                 for g in range(PASSES):
                     nc.tensor.matmul_mx(
@@ -121,7 +121,7 @@ def tile_ka_attention_heads_mod_pa_kernel(
 
         def copy_out(kc, k, e, ps):
             if (k, e) == (0, 0):
-                x_t[kc] = work.tile([P, 5 * H * POS, 4, B], F32, name="x_t")
+                x_t[kc] = work.tile([P, 5 * H * POS, 4, B], F32, name="x_t", bufs=1)
             col = 12 * k + 3 * e + kc
             nc.scalar.activation(
                 out=x_t[kc][:, k : 5 * H * POS : 5, e, :],
@@ -143,6 +143,19 @@ def tile_ka_attention_heads_mod_pa_kernel(
             pend = (k, e, ps)
         copy_out(0, *pend)
 
+        x_o = {}
+
+        def reorder(kc, j, a):
+            if a == 0:
+                x_o[kc, j] = work.tile([P, 12 * P], F32, name="x_o", bufs=5)
+            nc.scalar.copy(
+                out=x_o[kc, j][:, P * a : P * (a + 1)].rearrange("p (b h i) -> p h b i", b=B, i=4),
+                in_=x_t[kc][:, 96 * j + POS * a : 96 * j + POS * (a + 1), :, :].rearrange("p h i b -> p h b i"),
+            )
+
+        for a in range(12):
+            reorder(0, 0, a)
+
         ph, cps, csb, acc, ft, fp, sh, shx, x_ps = {}, {}, {}, {}, {}, {}, {}, {}, {}
 
         def pieces(i):
@@ -153,14 +166,12 @@ def tile_ka_attention_heads_mod_pa_kernel(
             ph[i] = work.tile([P, 12 * P], I32, name="phase", bufs=4)
             for a0, a1 in pieces(i):
                 nc.gpsimd.tensor_scalar(
-                    out=ph[i][:, P * a0 : P * a1].rearrange("p (a b c) -> p a b c", b=B, c=BLK),
-                    in0=x_t[kc][:, 96 * j + POS * a0 : 96 * j + POS * a1, :, :].rearrange(
-                        "p (a q) e b -> p a b (q e)", q=POS
-                    ),
+                    out=ph[i][:, P * a0 : P * a1],
+                    in0=x_o[kc, j][:, P * a0 : P * a1],
                     scalar1=turns[:, NF * j + m : NF * j + m + 1],
-                    scalar2=0.0,
+                    scalar2=1.0,
                     op0=ALU.mult,
-                    op1=ALU.add,
+                    op1=ALU.mult,
                 )
 
         def step_reduce(i):
@@ -176,16 +187,14 @@ def tile_ka_attention_heads_mod_pa_kernel(
                     op1=ALU.subtract,
                 )
 
-        def load_x(i, thirds):
+        def load_x(i):
             kc, j, m = steps[i]
-            for q in thirds:
-                x_ps[i // NF, q] = psum.tile([P, 512], F32, name="xp", bufs=4)
+            for q in range(3):
+                x_ps[i // NF, q] = psum.tile([P, 512], F32, name="xp", bufs=3)
                 nc.tensor.matmul(
-                    out=x_ps[i // NF, q][:].rearrange("p (a b c) -> p a b c", b=B, c=BLK),
+                    out=x_ps[i // NF, q][:],
                     lhsT=ident_f[:],
-                    rhs=x_t[kc][:, 96 * j + 32 * q : 96 * j + 32 * (q + 1), :, :].rearrange(
-                        "p (a q) e b -> p a b (q e)", q=POS
-                    ),
+                    rhs=x_o[kc, j][:, 512 * q : 512 * (q + 1)],
                     start=True,
                     stop=True,
                 )
@@ -197,7 +206,7 @@ def tile_ka_attention_heads_mod_pa_kernel(
 
         def step_coef(i):
             kc, j, m = steps[i]
-            cps[i] = psum.tile([P, 3 * P], BF16, name="coef_ps", bufs=2)
+            cps[i] = psum.tile([P, 4 * P], BF16, name="coef_ps", bufs=2)
             for q in range(3):
                 nc.tensor.transpose(cps[i][:, P * q : P * (q + 1)], coef_t[kc, q][:, :, m, j], ident_b[:])
 
@@ -205,7 +214,7 @@ def tile_ka_attention_heads_mod_pa_kernel(
 
         def copy_coef(i):
             csb[i] = work.tile([P, n_p], BF16, name="csb", bufs=2)
-            nc.scalar.copy(out=csb[i][:], in_=cps[i][:, n_v:])
+            nc.scalar.copy(out=csb[i][:], in_=cps[i][:, n_v : 3 * P])
 
         def step_mult(i):
             ft[i] = work.tile([P, B * n_v], F32, name="feat_v", bufs=2)
@@ -228,7 +237,7 @@ def tile_ka_attention_heads_mod_pa_kernel(
         def step_sum(i):
             kc, j, m = steps[i]
             if m % 2 == 0:
-                acc[i // 2] = psum.tile([P, 3, P], F32, name="acc", bufs=1)
+                acc[i // 2] = psum.tile([P, 3, P], F32, name="acc", bufs=2)
             for a in range(12):
                 s = (m % 2) * 12 + a
                 if s % 8 == 0:
@@ -259,16 +268,14 @@ def tile_ka_attention_heads_mod_pa_kernel(
                     in_=shift_v[kc, :, 12 * j + r : 12 * (j + 1) : 4, :],
                 )
 
-        def turn_shift(n):
-            sps = psum.tile([P, P], BF16, name="xl", bufs=1)
-            nc.tensor.transpose(sps[:], sh[n // 3][:, n % 3, :], ident_b[:])
-            return sps
+        def turn_shift(n, i):
+            nc.tensor.transpose(cps[i][:, 3 * P :], sh[n // 3][:, n % 3, :], ident_b[:])
 
-        def spread_shift(n, sps):
+        def spread_shift(n, i):
             shx[n] = work.tile([P, 4, B, BLK], F32, name="shx", bufs=2)
             nc.scalar.activation(
                 out=shx[n][:],
-                in_=sps[:].rearrange("p (o c) -> p o c", c=BLK).unsqueeze(2).to_broadcast([P, 4, B, BLK]),
+                in_=cps[i][:, 3 * P :].rearrange("p (o c) -> p o c", c=BLK).unsqueeze(2).to_broadcast([P, 4, B, BLK]),
                 func=ACT.Copy,
                 scale=1.0,
             )
@@ -281,51 +288,54 @@ def tile_ka_attention_heads_mod_pa_kernel(
             for b in range(B):
                 nc.sync.dma_start(out=out_v[b, kc, :, o0 : o0 + 3, :], in_=osb_t[BLK * b : BLK * (b + 1), :, :])
 
-        n_quads = n_steps * 12 // 32
-        shift_at = {(32 * n) // 12 - 3: n for n in range(n_quads)}
-        project_at = {}
-        for kc in range(1, KC):
-            free = [i for i in range(40 * (kc - 1), 40 * kc - 5) if i not in shift_at]
+        shift_at = {max((32 * n) // 12 - 1, 0): n for n in range(n_steps * 12 // 32)}
+        project_at, reorder_at = {}, {}
+        for kc in range(KC):
+            first = NF * G * kc
             for n in range(len(blocks)):
-                project_at[free[n]] = (kc,) + blocks[n]
-        x_pend, s_pend = None, None
-        for i in range(-4, n_steps + 1):
+                if kc > 0:
+                    project_at[first - 28 + n] = (kc,) + blocks[n]
+            for n in range(5 * 12):
+                if n >= 12 or kc > 0:
+                    reorder_at.setdefault(first - 3 + n // 4 - 3 * (kc > 0), []).append((kc, n // 12, n % 12))
+        x_pend = None
+        load_shift(0)
+        for i in range(-3, n_steps + 1):
             if 0 <= i < n_steps:
                 kc, j, m = steps[i]
                 if j == 0 and m == 0 and kc + 1 < KC:
                     load_coef(kc + 1)
-            if i == -4:
-                load_shift(0)
             if i >= 0 and i % 8 == 0 and i + 8 < n_steps:
                 load_shift(i // 8 + 1)
+            if i + 3 < n_steps:
+                step_round(i + 3)
             if 0 <= i < n_steps:
                 step_mult_p(i)
-            if 0 <= i + 3 < n_steps:
-                step_round(i + 3)
-            if i == -2:
-                load_x(0, range(3))
+            if i == -3:
+                load_x(0)
             if 0 <= i + 1 < n_steps:
                 step_coef(i + 1)
-                step_reduce(i + 1)
+                if i + 1 in shift_at:
+                    turn_shift(shift_at[i + 1], i + 1)
+            if 0 <= i + 2 < n_steps:
+                step_reduce(i + 2)
             if x_pend is not None:
                 copy_out(*x_pend)
                 x_pend = None
-            if s_pend is not None:
-                spread_shift(*s_pend)
-                s_pend = None
+            for r in reorder_at.get(i, []):
+                reorder(*r)
             if i >= 2 and i % 2 == 0:
                 finish(i // 2 - 1)
             if 0 <= i + 1 < n_steps:
                 copy_coef(i + 1)
-                step_sine(i + 1)
-            if i in shift_at:
-                s_pend = (shift_at[i], turn_shift(shift_at[i]))
+                if i + 1 in shift_at:
+                    spread_shift(shift_at[i + 1], i + 1)
+            if 0 <= i + 2 < n_steps:
+                step_sine(i + 2)
             if i in project_at:
                 x_pend = project_at[i] + (project(*project_at[i]),)
             if 0 <= i < n_steps:
-                if i + 2 < n_steps and steps[i + 2][2] == 0:
-                    load_x(i + 2, range(1, 3))
                 if i + 3 < n_steps and steps[i + 3][2] == 0:
-                    load_x(i + 3, range(1))
+                    load_x(i + 3)
                 step_mult(i)
                 step_sum(i)

import math
from contextlib import ExitStack

import concourse.mybir as mybir
from concourse.masks import make_identity

B, H, POS, D, NF, G = 4, 12, 8, 1536, 8, 5
TOK = B * H * POS
FLOPS = 2 * TOK * D * G * D + 4 * B * G * NF * D * H * POS

F32 = mybir.dt.float32
BF16 = mybir.dt.bfloat16
I32 = mybir.dt.int32
U8 = mybir.dt.uint8
FP4X4 = mybir.dt.float4_e2m1fn_x4
ALU = mybir.AluOpType
ACT = mybir.ActivationFunctionType

P = 128
PASSES = D // 512
KC = 3
BLK = 32
W_CHUNKS = ((0, 1), (1, 2), (2, 3), (3, 4), (4, 5))
A_V = 10


def tile_ka_attention_heads_mod_pa_kernel(
    tc, x_words, x_scales, lin_w_words, lin_w_scales, lin_b, grid, coef, shift, out
):
    nc = tc.nc
    steps = [(kc, j, m) for kc in range(KC) for j in range(G) for m in range(NF)]
    n_steps = len(steps)
    out_v = out.rearrange("b h g p d -> b (h g) (p d)").rearrange("b o (pe k l) -> b k pe o l", k=KC, l=P)
    shift_v = shift.rearrange("u h g p d -> (u h g) (p d)").rearrange("o (pe k l) -> k pe o l", k=KC, l=P)
    coef_v = coef.rearrange("(q a pe k l) m j -> k q (a pe) (l m j)", q=3, a=4, pe=BLK, k=KC, l=P)

    with ExitStack() as ctx:
        keep = ctx.enter_context(tc.tile_pool(name="keep", bufs=1))
        work = ctx.enter_context(tc.tile_pool(name="work", bufs=2))
        psum = ctx.enter_context(tc.psum_pool(name="psum", bufs=2))
        ctx.enter_context(tc.manual_schedule())

        x_codes = keep.tile([P, PASSES, 2 * TOK], U8, align_bytes=64, name="x_codes")
        x_planes = keep.tile([P, PASSES, TOK], U8, align_bytes=64, name="x_planes")
        w_codes, w_planes = [], []
        for ch, (k0, k1) in enumerate(W_CHUNKS):
            w_codes.append(keep.tile([P, PASSES, (k1 - k0) * 2 * D], U8, align_bytes=64, name="w_codes%d" % ch))
            w_planes.append(keep.tile([P, PASSES, (k1 - k0) * D], U8, align_bytes=64, name="w_planes%d" % ch))
        nc.gpsimd.memset(w_planes[0][:].bitcast(I32), 0)
        nc.vector.memset(x_planes[:].bitcast(I32), 0)
        for ch in range(1, len(W_CHUNKS)):
            nc.vector.memset(w_planes[ch][:].bitcast(I32), 0)

        def load_scales(planes, src, c0, c1, quads=range(4)):
            for q in quads:
                nc.sync.dma_start(
                    out=planes[32 * q : 32 * q + 4, :, :].bitcast(I32),
                    in_=src[:, 4 * q : 4 * q + 4, c0:c1].rearrange("g r n -> r g n").bitcast(I32),
                )

        nc.sync.dma_start(out=x_codes[:].bitcast(I32), in_=x_words.rearrange("g p n -> p g n").bitcast(I32))
        load_scales(x_planes, x_scales, 0, TOK)
        for ch, (k0, k1) in enumerate(W_CHUNKS):
            if ch == 0:
                load_scales(w_planes[ch], lin_w_scales, k0 * D, k1 * D, range(2))
            nc.sync.dma_start(
                out=w_codes[ch][:].bitcast(I32),
                in_=lin_w_words[:, :, k0 * 2 * D : k1 * 2 * D].rearrange("g p n -> p g n").bitcast(I32),
            )
            load_scales(w_planes[ch], lin_w_scales, k0 * D, k1 * D, range(2, 4) if ch == 0 else range(4))

        coef_t = {}

        def load_coef(kc):
            for q in range(3):
                t = work.tile([P, P, NF, G], BF16, name="coef%d" % q)
                nc.sync.dma_start(out=t[:].rearrange("p l m j -> p (l m j)"), in_=coef_v[kc, q])
                coef_t[kc, q] = t

        load_coef(0)

        ident_b = keep.tile([P, P], BF16, name="ident_b")
        make_identity(nc, ident_b[:])
        ident_f = keep.tile([P, P], F32, name="ident_f")
        make_identity(nc, ident_f[:])

        grid_b = keep.tile([P, G * NF], BF16, name="grid_b")
        nc.gpsimd.dma_start(out=grid_b[:], in_=grid.rearrange("j m -> (j m)").partition_broadcast(P))
        bias_rows = keep.tile([P, P], BF16, name="bias_rows")
        nc.vector.memset(bias_rows[:], 0.0)
        n_blk = G * D // P
        nc.gpsimd.dma_start(out=bias_rows[0:n_blk, :], in_=lin_b.rearrange("(c p) -> c p", p=P))
        turns = keep.tile([P, G * NF], F32, name="turns")
        nc.vector.tensor_scalar(
            out=turns[:], in0=grid_b[:], scalar1=1.0 / (2.0 * math.pi), scalar2=None, op0=ALU.mult
        )
        bias_ps = psum.tile([P, P], BF16, name="coef_ps", bufs=2)
        warm = keep.tile([P, 1], F32, name="warm")
        nc.vector.memset(warm[:], 0.0)
        nc.scalar.activation(out=warm[:], in_=warm[:], func=ACT.Sin, scale=1.0)
        bias = keep.tile([P, n_blk], F32, name="bias")

        x_t = {}

        def project(kc, k, e, bank="xl"):
            ch = [c for c, (k0, k1) in enumerate(W_CHUNKS) if k0 <= k < k1][0]
            blk = 12 * (k - W_CHUNKS[ch][0]) + 3 * e + kc
            ps = psum.tile([P, TOK], F32, name=bank, bufs=3 if bank == "xp" else 1)
            for t0, t1 in ((0, 256), (256, 384)):
                for g in range(PASSES):
                    nc.tensor.matmul_mx(
                        out=ps[:, t0:t1],
                        lhsT=w_codes[ch][:, g, 2 * P * blk : 2 * P * (blk + 1)].bitcast(FP4X4),
                        lhsT_scale=w_planes[ch][:, g, P * blk : P * (blk + 1)],
                        rhs=x_codes[:, g, 2 * t0 : 2 * t1].bitcast(FP4X4),
                        rhs_scale=x_planes[:, g, t0:t1],
                        start=(g == 0),
                        stop=(g == PASSES - 1),
                    )
            return ps

        def copy_out(kc, k, e, ps):
            if (k, e) == (0, 0):
                x_t[kc] = work.tile([P, 5 * H * POS, 4, B], F32, name="x_t", bufs=1)
            col = 12 * k + 3 * e + kc
            nc.scalar.activation(
                out=x_t[kc][:, k : 5 * H * POS : 5, e, :],
                in_=ps[:].rearrange("p (b r) -> p r b", b=B),
                func=ACT.Identity,
                bias=bias[:, col : col + 1],
                scale=1.0,
            )

        blocks = [(k, e) for k in range(5) for e in range(4)]
        pend = None
        for k, e in blocks:
            ps = project(0, k, e, "xl" if e == 0 else "xp")
            if (k, e) == (0, 1):
                nc.tensor.transpose(bias_ps[:], bias_rows[:], ident_b[:])
                nc.vector.tensor_copy(out=bias[:], in_=bias_ps[:, 0:n_blk])
            if pend is not None:
                copy_out(0, *pend)
            pend = (k, e, ps)
        copy_out(0, *pend)

        x_o = {}

        def reorder(kc, j, a):
            if a == 0:
                x_o[kc, j] = work.tile([P, 12 * P], F32, name="x_o", bufs=5)
            nc.scalar.copy(
                out=x_o[kc, j][:, P * a : P * (a + 1)].rearrange("p (b h i) -> p h b i", b=B, i=4),
                in_=x_t[kc][:, 96 * j + POS * a : 96 * j + POS * (a + 1), :, :].rearrange("p h i b -> p h b i"),
            )

        for a in range(12):
            reorder(0, 0, a)

        ph, cps, csb, acc, ft, fp, sh, shx, x_ps = {}, {}, {}, {}, {}, {}, {}, {}, {}

        def pieces(i):
            return ((0, 4), (4, 8), (8, 12)) if i == 0 else ((0, 12),)

        def step_round(i):
            kc, j, m = steps[i]
            ph[i] = work.tile([P, 12 * P], I32, name="phase", bufs=4)
            for a0, a1 in pieces(i):
                nc.gpsimd.tensor_scalar(
                    out=ph[i][:, P * a0 : P * a1],
                    in0=x_o[kc, j][:, P * a0 : P * a1],
                    scalar1=turns[:, NF * j + m : NF * j + m + 1],
                    scalar2=1.0,
                    op0=ALU.mult,
                    op1=ALU.mult,
                )

        def step_reduce(i):
            kc, j, m = steps[i]
            for q in range(3):
                cols = slice(512 * q, 512 * (q + 1))
                nc.vector.scalar_tensor_tensor(
                    out=ph[i][:, cols].bitcast(F32),
                    in0=x_ps[i // NF, q][:],
                    scalar=turns[:, NF * j + m : NF * j + m + 1],
                    in1=ph[i][:, cols],
                    op0=ALU.mult,
                    op1=ALU.subtract,
                )

        def load_x(i):
            kc, j, m = steps[i]
            for q in range(3):
                x_ps[i // NF, q] = psum.tile([P, 512], F32, name="xp", bufs=3)
                nc.tensor.matmul(
                    out=x_ps[i // NF, q][:],
                    lhsT=ident_f[:],
                    rhs=x_o[kc, j][:, 512 * q : 512 * (q + 1)],
                    start=True,
                    stop=True,
                )

        def step_sine(i):
            for a0, a1 in pieces(i):
                v = ph[i][:, P * a0 : P * a1].bitcast(F32)
                nc.scalar.activation(out=v, in_=v, func=ACT.Sin, scale=2.0 * math.pi)

        def step_coef(i):
            kc, j, m = steps[i]
            cps[i] = psum.tile([P, 4 * P], BF16, name="coef_ps", bufs=2)
            for q in range(3):
                nc.tensor.transpose(cps[i][:, P * q : P * (q + 1)], coef_t[kc, q][:, :, m, j], ident_b[:])

        n_v, n_p = BLK * A_V, BLK * (12 - A_V)

        def copy_coef(i):
            csb[i] = work.tile([P, n_p], BF16, name="csb", bufs=2)
            nc.scalar.copy(out=csb[i][:], in_=cps[i][:, n_v : 3 * P])

        def step_mult(i):
            ft[i] = work.tile([P, B * n_v], F32, name="feat_v", bufs=2)
            nc.vector.tensor_tensor(
                out=ft[i][:].rearrange("p (a b c) -> p a b c", b=B, c=BLK),
                in0=ph[i][:, 0 : B * n_v].bitcast(F32).rearrange("p (a b c) -> p a b c", b=B, c=BLK),
                in1=cps[i][:, 0:n_v].rearrange("p (a c) -> p a c", c=BLK).unsqueeze(2).to_broadcast([P, A_V, B, BLK]),
                op=ALU.mult,
            )

        def step_mult_p(i):
            fp[i] = work.tile([P, B * n_p], F32, name="feat_p", bufs=2)
            nc.gpsimd.tensor_tensor(
                out=fp[i][:].rearrange("p (a b c) -> p a b c", b=B, c=BLK),
                in0=ph[i][:, B * n_v :].bitcast(F32).rearrange("p (a b c) -> p a b c", b=B, c=BLK),
                in1=csb[i][:].rearrange("p (a c) -> p a c", c=BLK).unsqueeze(2).to_broadcast([P, 12 - A_V, B, BLK]),
                op=ALU.mult,
            )

        def step_sum(i):
            kc, j, m = steps[i]
            if m % 2 == 0:
                acc[i // 2] = psum.tile([P, 3, P], F32, name="acc", bufs=2)
            for a in range(12):
                s = (m % 2) * 12 + a
                if s % 8 == 0:
                    o = (12 * i + a) // 8
                    nc.tensor.matmul(
                        out=acc[i // 2][:, s // 8, :],
                        lhsT=shx[o // 4][:, o % 4, :, :].rearrange("p b c -> p (b c)"),
                        rhs=ident_f[:],
                        is_transpose=True,
                        start=True,
                        stop=False,
                    )
                nc.tensor.matmul(
                    out=acc[i // 2][:, s // 8, :],
                    lhsT=ft[i][:, P * a : P * (a + 1)] if a < A_V else fp[i][:, P * (a - A_V) : P * (a - A_V + 1)],
                    rhs=ident_f[:],
                    is_transpose=True,
                    start=False,
                    stop=(s % 8 == 7),
                )

        def load_shift(n):
            sh[n] = work.tile([P, 3, P], BF16, name="sh", bufs=2)
            kc, j = divmod(n, G)
            for r in range(4):
                nc.sync.dma_start(
                    out=sh[n][BLK * r : BLK * (r + 1), :, :],
                    in_=shift_v[kc, :, 12 * j + r : 12 * (j + 1) : 4, :],
                )

        def turn_shift(n, i):
            nc.tensor.transpose(cps[i][:, 3 * P :], sh[n // 3][:, n % 3, :], ident_b[:])

        def spread_shift(n, i):
            shx[n] = work.tile([P, 4, B, BLK], F32, name="shx", bufs=2)
            nc.scalar.activation(
                out=shx[n][:],
                in_=cps[i][:, 3 * P :].rearrange("p (o c) -> p o c", c=BLK).unsqueeze(2).to_broadcast([P, 4, B, BLK]),
                func=ACT.Copy,
                scale=1.0,
            )

        def finish(tr):
            kc, j, m = steps[2 * tr]
            o0 = 12 * j + 3 * (m // 2)
            osb_t = work.tile([P, 3, P], F32, name="osb", bufs=2)
            nc.scalar.copy(out=osb_t[:], in_=acc[tr][:])
            for b in range(B):
                nc.sync.dma_start(out=out_v[b, kc, :, o0 : o0 + 3, :], in_=osb_t[BLK * b : BLK * (b + 1), :, :])

        shift_at = {max((32 * n) // 12 - 1, 0): n for n in range(n_steps * 12 // 32)}
        project_at, reorder_at = {}, {}
        for kc in range(KC):
            first = NF * G * kc
            for n in range(len(blocks)):
                if kc > 0:
                    project_at[first - 28 + n] = (kc,) + blocks[n]
            for n in range(5 * 12):
                if n >= 12 or kc > 0:
                    reorder_at.setdefault(first - 3 + n // 4 - 3 * (kc > 0), []).append((kc, n // 12, n % 12))
        x_pend = None
        load_shift(0)
        for i in range(-3, n_steps + 1):
            if 0 <= i < n_steps:
                kc, j, m = steps[i]
                if j == 0 and m == 0 and kc + 1 < KC:
                    load_coef(kc + 1)
            if i >= 0 and i % 8 == 0 and i + 8 < n_steps:
                load_shift(i // 8 + 1)
            if i + 3 < n_steps:
                step_round(i + 3)
            if 0 <= i < n_steps:
                step_mult_p(i)
            if i == -3:
                load_x(0)
            if 0 <= i + 1 < n_steps:
                step_coef(i + 1)
                if i + 1 in shift_at:
                    turn_shift(shift_at[i + 1], i + 1)
            if 0 <= i + 2 < n_steps:
                step_reduce(i + 2)
            if x_pend is not None:
                copy_out(*x_pend)
                x_pend = None
            for r in reorder_at.get(i, []):
                reorder(*r)
            if i >= 2 and i % 2 == 0:
                finish(i // 2 - 1)
            if 0 <= i + 1 < n_steps:
                copy_coef(i + 1)
                if i + 1 in shift_at:
                    spread_shift(shift_at[i + 1], i + 1)
            if 0 <= i + 2 < n_steps:
                step_sine(i + 2)
            if i in project_at:
                x_pend = project_at[i] + (project(*project_at[i]),)
            if 0 <= i < n_steps:
                if i + 3 < n_steps and steps[i + 3][2] == 0:
                    load_x(i + 3)
                step_mult(i)
                step_sum(i)
